import numpy as np
import ml_dtypes


def mxq(x, axis, fmt="e4m3"):
    dtype, down = {"e4m3": (ml_dtypes.float8_e4m3fn, 7), "e5m2": (ml_dtypes.float8_e5m2, 14)}[fmt]
    v = np.moveaxis(np.asarray(x, np.float32).astype(ml_dtypes.bfloat16).astype(np.float64), axis, -1)
    blocks = v.reshape(v.shape[:-1] + (-1, 32))
    amax = np.abs(blocks).max(-1, keepdims=True)
    byte = np.maximum(np.where(amax > 0, np.frexp(amax)[1] - 1 + 127, 0) - down, 1)
    scale = np.exp2(byte - 127.0)
    codes = (blocks / scale).astype(np.float32).astype(dtype).astype(np.float64)
    return np.moveaxis((codes * scale).reshape(v.shape), -1, axis)


WIDE = False


def mx_kscale(k):
    if not WIDE:
        return np.ones(k)
    levels = np.array([10, -10, 5, -5, 0])
    if k % 512:
        return np.exp2(np.random.permutation(np.resize(levels, k // 32))).repeat(32)
    a = np.empty((k // 512, 16))
    for p in range(k // 512):
        a[p, :8] = np.random.permutation(np.resize(levels, 8))
        for g in range(8):
            far = levels[np.abs(levels - a[p, g]) >= 10]
            a[p, g + 8] = far[np.random.randint(len(far))]
    return np.exp2(a.ravel()).repeat(32)


BF16 = ml_dtypes.bfloat16


def bf(x):
    return np.asarray(x, np.float32).astype(BF16)


def f64(x):
    return np.asarray(x).astype(np.float64)


B, N, F_IN, F_OUT, K = 4, 2048, 128, 256, 4


def setup_inputs():
    s = mx_kscale(N)
    r = (s.min() / s)[:, None]
    return {"x": bf(np.random.standard_normal((B, N, F_IN)) * r),
            "L": bf(np.random.standard_normal((N, N)) * 0.7 / np.sqrt(N) * s[None, :] / s[:, None])}


def reference(x, L):
    Lq = mxq(f64(L), 1, "e4m3")
    x1 = Lq @ mxq(f64(x), 1, "e4m3")
    x2 = Lq @ mxq(x1, 1, "e4m3")
    xt2 = 2.0 * x2 - f64(x)
    return x1, x2, xt2

@@ -1,0 +1,274 @@
+from contextlib import ExitStack
+
+import concourse.mybir as mybir
+from concourse.masks import make_identity
+
+F32 = mybir.dt.float32
+BF16 = mybir.dt.bfloat16
+U32 = mybir.dt.uint32
+U8 = mybir.dt.uint8
+FP8X4 = mybir.dt.float8_e4m3fn_x4
+MULT = mybir.AluOpType.mult
+SUB = mybir.AluOpType.subtract
+
+P = 128
+B, N, F = 4, 2048, 128
+NI = N // 256
+NG = N // 512
+FLOPS = 2 * 2 * N * N * B * F
+
+
+def tile_gcncheb_pa_kernel(tc, x, L, out_0, out_1, out_2):
+    nc = tc.nc
+    with ExitStack() as ctx:
+        ctx.enter_context(tc.manual_schedule())
+        keep = ctx.enter_context(tc.tile_pool(name="keep", bufs=1))
+        lgp = ctx.enter_context(tc.tile_pool(name="lgp", bufs=4))
+        xgp = ctx.enter_context(tc.tile_pool(name="xgp", bufs=2))
+        x1gp = ctx.enter_context(tc.tile_pool(name="x1gp", bufs=2))
+        st1p = ctx.enter_context(tc.tile_pool(name="st1p", bufs=4))
+        st2p = ctx.enter_context(tc.tile_pool(name="st2p", bufs=8))
+        st3p = ctx.enter_context(tc.tile_pool(name="st3p", bufs=8))
+        psum = ctx.enter_context(tc.psum_pool(name="psum", bufs=1))
+
+        def bank(k, shape):
+            return psum.tile(shape, F32, name="bank%d" % k, tag="bank%d" % k)
+
+        ident = keep.tile([P, P], F32, name="ident")
+        make_identity(nc, ident[:])
+
+        lraw = [keep.tile([P, 2, N], BF16, name="lraw%d" % i) for i in range(NI)]
+        xraw = keep.tile([P, B, N], BF16, name="xraw")
+        ltc = keep.tile([P, NI, 2, 512], U32, name="ltc", align_bytes=64)
+        lts = keep.tile([P, NI, 2, 512], U8, name="lts", align_bytes=64)
+        xqc = keep.tile([P, 2, NG, 256], U32, name="xqc", align_bytes=64)
+        xqs = keep.tile([P, 2, NG, 256], U8, name="xqs", align_bytes=64)
+        yqc = keep.tile([P, 2, NG, 256], U32, name="yqc", align_bytes=64)
+        yqs = keep.tile([P, 2, NG, 256], U8, name="yqs", align_bytes=64)
+
+        def load_l(i):
+            nc.sync.dma_start(
+                out=lraw[i][:],
+                in_=L[512 * (i // 2) : 512 * (i // 2) + 512, :].rearrange(
+                    "(p w e) b -> p w e b", w=2, e=2
+                )[:, i % 2],
+            )
+
+        def load_x(c):
+            nc.sync.dma_start(
+                out=xraw[:, c, :].rearrange("p (g t f) -> p g t f", t=4, f=F),
+                in_=x[c].rearrange("(g p t) f -> p g t f", p=P, t=4),
+            )
+
+        load_l(0)
+        load_x(0)
+        load_x(1)
+        for i in range(1, NI):
+            load_l(i)
+        load_x(2)
+        load_x(3)
+
+        def warm(c, k):
+            w = bank(k, [P, 512])
+            for r in range(3):
+                nc.tensor.matmul(
+                    out=w[:], lhsT=xraw[:, c, 0:P], rhs=xraw[:, c, 0:512], start=True, stop=True
+                )
+
+        xg_tiles = {}
+
+        def x_regroup(c):
+            h, c2 = divmod(c, 2)
+            if c2 == 0:
+                xg = xgp.tile([P, NG, 2, F, 4], BF16, name="xg", align_bytes=64)
+                xg_tiles[h] = xg
+            nc.vector.tensor_copy(
+                out=xg_tiles[h][:, :, c2, :, :],
+                in_=xraw[:, c, :].rearrange("p (g t f) -> p g f t", t=4, f=F),
+            )
+
+        def x_quant(h):
+            nc.vector.quantize_mx(
+                out=xqc[:, h].rearrange("p g w -> p (g w)").bitcast(FP8X4),
+                scales=xqs[:, h].rearrange("p g w -> p (g w)"),
+                in_=xg_tiles[h][:].rearrange("p g c f t -> p (g c f t)"),
+            )
+
+        lg_tiles = {}
+
+        def transposes(i, on_vector):
+            for e in range(2):
+                lw = lraw[i][:, e, :].bitcast(F32)
+                lg = lgp.tile([P, N], BF16, name="lg", align_bytes=64)
+                lg_tiles[(i, e)] = lg
+                lgw = lg[:].bitcast(F32).rearrange("p (g c u) -> p g c u", c=P, u=2)
+                for gg in range(2):
+                    tp = bank(2 * e + gg, [P, 4, P])
+                    for s in range(4):
+                        w0 = 512 * gg + 256 * (s // 2)
+                        nc.tensor.transpose(
+                            tp[:, s, :], lw[:, w0 + s % 2 : w0 + 256 : 2], ident[:]
+                        )
+                    src = tp[:].rearrange("p (g u) c -> p g c u", u=2)
+                    dst = lgw[:, 2 * gg : 2 * gg + 2, :, :]
+                    if 2 * e + gg in on_vector:
+                        nc.vector.tensor_copy(out=dst, in_=src)
+                    else:
+                        nc.scalar.copy(out=dst, in_=src)
+
+        def l_quant(i):
+            for e in range(2):
+                nc.vector.quantize_mx(
+                    out=ltc[:, i, e, :].bitcast(FP8X4),
+                    scales=lts[:, i, e, :],
+                    in_=lg_tiles[(i, e)][:],
+                )
+
+        def one_pass(out, i, e, g, h, rc, rs):
+            nc.tensor.matmul_mx(
+                out=out,
+                lhsT=ltc[:, i, e, P * g : P * g + P].bitcast(FP8X4),
+                lhsT_scale=lts[:, i, e, P * g : P * g + P],
+                rhs=rc[:, h, g, :].bitcast(FP8X4),
+                rhs_scale=rs[:, h, g, :],
+                start=(g == 0),
+                stop=(g == NG - 1),
+            )
+
+        def passes(k, i, h, rc, rs):
+            acc = bank(k, [P, 2, 256])
+            for e in range(2):
+                for g in range(NG):
+                    one_pass(acc[:, e, :], i, e, g, h, rc, rs)
+            return acc
+
+        def dram_rows(o, i, h):
+            g0 = 512 * (i // 2)
+            return o[2 * h : 2 * h + 2, g0 : g0 + 512, :].rearrange(
+                "c (p w e) f -> p c w e f", w=2, e=2
+            )[:, :, i % 2]
+
+        def split_ef(ap):
+            return ap.rearrange("p c (e f) -> p c e f", e=2)
+
+        st1_tiles = {}
+
+        def hop1_out(i, h, acc):
+            gq, u = divmod(i, 2)
+            if u == 0:
+                st1 = st1p.tile([P, 2, 512], F32, name="st1")
+                st1_tiles[(gq, h)] = st1
+            part = split_ef(st1_tiles[(gq, h)][:, :, 256 * u : 256 * u + 256])
+            nc.scalar.copy(out=part, in_=acc[:].rearrange("p e (c f) -> p c e f", c=2))
+            nc.sync.dma_start(out=dram_rows(out_0, i, h), in_=part)
+
+        def hop1_quant(gq, h):
+            x1g = x1gp.tile([P, 2, F, 4], BF16, name="x1g", align_bytes=64)
+            nc.vector.tensor_copy(
+                out=x1g[:],
+                in_=st1_tiles[(gq, h)][:].rearrange("p c (t f) -> p c f t", t=4),
+            )
+            nc.vector.quantize_mx(
+                out=yqc[:, h, gq, :].bitcast(FP8X4),
+                scales=yqs[:, h, gq, :],
+                in_=x1g[:].rearrange("p c f t -> p (c f t)"),
+            )
+
+        def hop2_x2(i, h, accs):
+            st2 = st2p.tile([P, 2, 256], F32, name="st2")
+            if len(accs) == 1:
+                nc.scalar.copy(
+                    out=split_ef(st2[:]), in_=accs[0][:].rearrange("p e (c f) -> p c e f", c=2)
+                )
+            else:
+                for e in range(2):
+                    nc.scalar.copy(
+                        out=split_ef(st2[:])[:, :, e, :],
+                        in_=accs[e][:].rearrange("p (c f) -> p c f", c=2),
+                    )
+            nc.sync.dma_start(out=dram_rows(out_1, i, h), in_=split_ef(st2[:]))
+            return st2
+
+        def hop2_xt2(i, h, st2):
+            st3 = st3p.tile([P, 2, 256], F32, name="st3")
+            nc.vector.scalar_tensor_tensor(
+                out=st3[:],
+                in0=st2[:],
+                scalar=2.0,
+                in1=xraw[:, 2 * h : 2 * h + 2, 256 * i : 256 * i + 256],
+                op0=MULT,
+                op1=SUB,
+            )
+            nc.sync.dma_start(out=dram_rows(out_2, i, h), in_=split_ef(st3[:]))
+
+        transposes(0, ())
+        warm(0, 4)
+        warm(1, 5)
+        x_regroup(0)
+        l_quant(0)
+        x_regroup(1)
+        x_quant(0)
+        for i in range(NI):
+            if i + 1 < NI:
+                transposes(i + 1, (1, 3) if i + 1 == NI - 1 else (1,))
+            acc = passes(4 + i % 4, i, 0, xqc, xqs)
+            if i == NI - 2:
+                l_quant(i + 1)
+                hop1_quant(i // 2 - 1, 0)
+            else:
+                if i % 2 == 0 and i > 0:
+                    hop1_quant(i // 2 - 1, 0)
+                if i + 1 < NI:
+                    l_quant(i + 1)
+            hop1_out(i, 0, acc)
+
+        n_open = 3
+        opened = {}
+        for j in range(n_open):
+            opened[j] = []
+            for e in range(2):
+                acc = bank(2 * j + e, [P, 256])
+                for g in range(NG - 1):
+                    one_pass(acc[:], j, e, g, 0, yqc, yqs)
+                opened[j].append(acc)
+        hop1_quant(3, 0)
+        x_regroup(2)
+        st2_open = {}
+        for j in range(n_open):
+            for e in range(2):
+                one_pass(opened[j][e][:], j, e, NG - 1, 0, yqc, yqs)
+            st2_open[j] = hop2_x2(j, 0, opened[j])
+        x_regroup(3)
+        x_quant(1)
+        for j in range(n_open):
+            hop2_xt2(j, 0, st2_open[j])
+
+        rot = [2 * n_open]
+
+        def next_bank():
+            k = rot[0] % 8
+            rot[0] += 1
+            return k
+
+        def hop1_b(i):
+            acc = passes(next_bank(), i, 1, xqc, xqs)
+            hop1_out(i, 1, acc)
+            if i % 2 == 1:
+                hop1_quant(i // 2, 1)
+
+        def hop2(i, h):
+            acc = passes(next_bank(), i, h, yqc, yqs)
+            st2 = hop2_x2(i, h, [acc])
+            hop2_xt2(i, h, st2)
+
+        hop2(3, 0)
+        hop2(4, 0)
+        for i in range(NI):
+            hop1_b(i)
+            if i == NI - 2:
+                hop2(5, 0)
+        hop2(6, 0)
+        hop2(7, 0)
+
+        for j in range(NI):
+            hop2(j, 1)

@@ -1,8 +1,6 @@
 from contextlib import ExitStack
-
 import concourse.mybir as mybir
 from concourse.masks import make_identity
-
 F32 = mybir.dt.float32
 BF16 = mybir.dt.bfloat16
 U32 = mybir.dt.uint32
@@ -10,13 +8,19 @@ U8 = mybir.dt.uint8
 FP8X4 = mybir.dt.float8_e4m3fn_x4
 MULT = mybir.AluOpType.mult
 SUB = mybir.AluOpType.subtract
-
 P = 128
 B, N, F = 4, 2048, 128
 NI = N // 256
 NG = N // 512
 FLOPS = 2 * 2 * N * N * B * F
-
+SPLIT=False
+VEV=[1]
+LAG=99
+NOPEN=3
+XORDER=[["l",0],["x",0],["x",1],["l",1],["l",2],["l",3],["l",4],["l",5],["l",6],["l",7],["x",2],["x",3]]
+STG=2
+WARM=6
+BSEQ=[["b",3],["b",4],["b",5],["b",6],["a",0],["a",1],["a",2],["a",3],["a",4],["a",5],["a",6],["a",7],["b",7],["c",0],["c",1],["c",2],["c",3],["c",4],["c",5],["c",6],["c",7]]
 
 def tile_gcncheb_pa_kernel(tc, x, L, out_0, out_1, out_2):
     nc = tc.nc
@@ -27,16 +31,13 @@ def tile_gcncheb_pa_kernel(tc, x, L, out_0, out_1, out_2):
         xgp = ctx.enter_context(tc.tile_pool(name="xgp", bufs=2))
         x1gp = ctx.enter_context(tc.tile_pool(name="x1gp", bufs=2))
         st1p = ctx.enter_context(tc.tile_pool(name="st1p", bufs=4))
-        st2p = ctx.enter_context(tc.tile_pool(name="st2p", bufs=8))
-        st3p = ctx.enter_context(tc.tile_pool(name="st3p", bufs=8))
+        st2p = ctx.enter_context(tc.tile_pool(name="st2p", bufs=4))
+        st3p = ctx.enter_context(tc.tile_pool(name="st3p", bufs=4))
         psum = ctx.enter_context(tc.psum_pool(name="psum", bufs=1))
-
         def bank(k, shape):
             return psum.tile(shape, F32, name="bank%d" % k, tag="bank%d" % k)
-
         ident = keep.tile([P, P], F32, name="ident")
         make_identity(nc, ident[:])
-
         lraw = [keep.tile([P, 2, N], BF16, name="lraw%d" % i) for i in range(NI)]
         xraw = keep.tile([P, B, N], BF16, name="xraw")
         ltc = keep.tile([P, NI, 2, 512], U32, name="ltc", align_bytes=64)
@@ -46,37 +47,22 @@ def tile_gcncheb_pa_kernel(tc, x, L, out_0, out_1, out_2):
         yqc = keep.tile([P, 2, NG, 256], U32, name="yqc", align_bytes=64)
         yqs = keep.tile([P, 2, NG, 256], U8, name="yqs", align_bytes=64)
 
+        def lview(i):
+            return L[512 * (i // 2) : 512 * (i // 2) + 512, :].rearrange("(p w e) b -> p w e b", w=2, e=2)[:, i % 2]
         def load_l(i):
-            nc.sync.dma_start(
-                out=lraw[i][:],
-                in_=L[512 * (i // 2) : 512 * (i // 2) + 512, :].rearrange(
-                    "(p w e) b -> p w e b", w=2, e=2
-                )[:, i % 2],
-            )
-
+            nc.sync.dma_start(out=lraw[i][:], in_=lview(i))
+        def load_lh(i, e):
+            nc.sync.dma_start(out=lraw[i][:, e], in_=lview(i)[:, e])
         def load_x(c):
             nc.sync.dma_start(
                 out=xraw[:, c, :].rearrange("p (g t f) -> p g t f", t=4, f=F),
                 in_=x[c].rearrange("(g p t) f -> p g t f", p=P, t=4),
             )
-
-        load_l(0)
-        load_x(0)
-        load_x(1)
-        for i in range(1, NI):
-            load_l(i)
-        load_x(2)
-        load_x(3)
-
-        def warm(c, k):
-            w = bank(k, [P, 512])
-            for r in range(3):
-                nc.tensor.matmul(
-                    out=w[:], lhsT=xraw[:, c, 0:P], rhs=xraw[:, c, 0:512], start=True, stop=True
-                )
-
+        for k, n in XORDER:
+            if k == 'l': load_l(n)
+            elif k == 'x': load_x(n)
+            elif k == 'h': load_lh(n // 2, n % 2)
         xg_tiles = {}
-
         def x_regroup(c):
             h, c2 = divmod(c, 2)
             if c2 == 0:
@@ -86,44 +72,32 @@ def tile_gcncheb_pa_kernel(tc, x, L, out_0, out_1, out_2):
                 out=xg_tiles[h][:, :, c2, :, :],
                 in_=xraw[:, c, :].rearrange("p (g t f) -> p g f t", t=4, f=F),
             )
-
         def x_quant(h):
             nc.vector.quantize_mx(
                 out=xqc[:, h].rearrange("p g w -> p (g w)").bitcast(FP8X4),
                 scales=xqs[:, h].rearrange("p g w -> p (g w)"),
                 in_=xg_tiles[h][:].rearrange("p g c f t -> p (g c f t)"),
             )
-
         lg_tiles = {}
-
-        def transposes(i, on_vector):
-            for e in range(2):
-                lw = lraw[i][:, e, :].bitcast(F32)
-                lg = lgp.tile([P, N], BF16, name="lg", align_bytes=64)
-                lg_tiles[(i, e)] = lg
-                lgw = lg[:].bitcast(F32).rearrange("p (g c u) -> p g c u", c=P, u=2)
-                for gg in range(2):
-                    tp = bank(2 * e + gg, [P, 4, P])
-                    for s in range(4):
-                        w0 = 512 * gg + 256 * (s // 2)
-                        nc.tensor.transpose(
-                            tp[:, s, :], lw[:, w0 + s % 2 : w0 + 256 : 2], ident[:]
-                        )
-                    src = tp[:].rearrange("p (g u) c -> p g c u", u=2)
-                    dst = lgw[:, 2 * gg : 2 * gg + 2, :, :]
-                    if 2 * e + gg in on_vector:
-                        nc.vector.tensor_copy(out=dst, in_=src)
-                    else:
-                        nc.scalar.copy(out=dst, in_=src)
-
-        def l_quant(i):
-            for e in range(2):
-                nc.vector.quantize_mx(
-                    out=ltc[:, i, e, :].bitcast(FP8X4),
-                    scales=lts[:, i, e, :],
-                    in_=lg_tiles[(i, e)][:],
-                )
-
+        def transposes(i, e):
+            lw = lraw[i][:, e, :].bitcast(F32)
+            lg = lgp.tile([P, N], BF16, name="lg", align_bytes=64)
+            lg_tiles[(i, e)] = lg
+            lgw = lg[:].bitcast(F32).rearrange("p (g c u) -> p g c u", c=P, u=2)
+            for gg in range(2):
+                tp = bank(2 * e + gg, [P, 4, P])
+                for s in range(4):
+                    w0 = 512 * gg + 256 * (s // 2)
+                    src1 = lw[:, w0 + s % 2 : w0 + 256 : 2]
+                    nc.tensor.transpose(tp[:, s, :], src1, ident[:])
+                src = tp[:].rearrange("p (g u) c -> p g c u", u=2)
+                dst = lgw[:, 2 * gg : 2 * gg + 2, :, :]
+                if 2 * e + gg in VEV[i % len(VEV)] if isinstance(VEV[0], list) else 2 * e + gg in VEV:
+                    nc.vector.tensor_copy(out=dst, in_=src)
+                else:
+                    nc.scalar.copy(out=dst, in_=src)
+        def l_quant(i, e):
+            nc.vector.quantize_mx(out=ltc[:, i, e, :].bitcast(FP8X4), scales=lts[:, i, e, :], in_=lg_tiles[(i, e)][:])
         def one_pass(out, i, e, g, h, rc, rs):
             nc.tensor.matmul_mx(
                 out=out,
@@ -134,141 +108,157 @@ def tile_gcncheb_pa_kernel(tc, x, L, out_0, out_1, out_2):
                 start=(g == 0),
                 stop=(g == NG - 1),
             )
-
-        def passes(k, i, h, rc, rs):
-            acc = bank(k, [P, 2, 256])
-            for e in range(2):
-                for g in range(NG):
-                    one_pass(acc[:, e, :], i, e, g, h, rc, rs)
-            return acc
-
-        def dram_rows(o, i, h):
+        def passes_e(acc, i, e, h, rc, rs):
+            for g in range(NG):
+                one_pass(acc[:, e, :], i, e, g, h, rc, rs)
+        def dram_rows(o, g, h):
+            return o[2 * h : 2 * h + 2, 512 * g : 512 * g + 512, :].rearrange("c (p t) f -> p c (t f)", t=4)
+        def dram_rows_c(o, g, c):
+            return o[c, 512 * g : 512 * g + 512, :].rearrange("(p t) f -> p (t f)", t=4)
+        def dram_rows_w(o, i, h):
             g0 = 512 * (i // 2)
-            return o[2 * h : 2 * h + 2, g0 : g0 + 512, :].rearrange(
-                "c (p w e) f -> p c w e f", w=2, e=2
-            )[:, :, i % 2]
-
-        def split_ef(ap):
-            return ap.rearrange("p c (e f) -> p c e f", e=2)
-
+            return o[2 * h : 2 * h + 2, g0 : g0 + 512, :].rearrange("c (p w e) f -> p c w (e f)", w=2, e=2)[:, :, i % 2]
         st1_tiles = {}
-
         def hop1_out(i, h, acc):
             gq, u = divmod(i, 2)
             if u == 0:
                 st1 = st1p.tile([P, 2, 512], F32, name="st1")
                 st1_tiles[(gq, h)] = st1
-            part = split_ef(st1_tiles[(gq, h)][:, :, 256 * u : 256 * u + 256])
+            part = st1_tiles[(gq, h)][:, :, 256 * u : 256 * u + 256].rearrange("p c (e f) -> p c e f", e=2)
             nc.scalar.copy(out=part, in_=acc[:].rearrange("p e (c f) -> p c e f", c=2))
-            nc.sync.dma_start(out=dram_rows(out_0, i, h), in_=part)
-
-        def hop1_quant(gq, h):
+            if STG == 1:
+                nc.sync.dma_start(out=dram_rows_w(out_0, i, h), in_=st1_tiles[(gq, h)][:, :, 256 * u : 256 * u + 256])
+            elif u == 1:
+                nc.sync.dma_start(out=dram_rows(out_0, gq, h), in_=st1_tiles[(gq, h)][:])
+        x1g_tiles = {}
+        def hop1_regroup(gq, h):
             x1g = x1gp.tile([P, 2, F, 4], BF16, name="x1g", align_bytes=64)
-            nc.vector.tensor_copy(
-                out=x1g[:],
-                in_=st1_tiles[(gq, h)][:].rearrange("p c (t f) -> p c f t", t=4),
-            )
+            x1g_tiles[(gq, h)] = x1g
+            nc.vector.tensor_copy(out=x1g[:], in_=st1_tiles[(gq, h)][:].rearrange("p c (t f) -> p c f t", t=4))
+        def hop1_q(gq, h):
             nc.vector.quantize_mx(
                 out=yqc[:, h, gq, :].bitcast(FP8X4),
                 scales=yqs[:, h, gq, :],
-                in_=x1g[:].rearrange("p c f t -> p (c f t)"),
+                in_=x1g_tiles[(gq, h)][:].rearrange("p c f t -> p (c f t)"),
             )
-
+        def hop1_quant(gq, h):
+            hop1_regroup(gq, h)
+            hop1_q(gq, h)
+        st2_tiles = {}
         def hop2_x2(i, h, accs):
-            st2 = st2p.tile([P, 2, 256], F32, name="st2")
+            g, u = divmod(i, 2)
+            if u == 0:
+                st2 = st2p.tile([P, 2, 512], F32, name="st2")
+                st3 = st3p.tile([P, 2, 512], F32, name="st3")
+                st2_tiles[(g, h)] = (st2, st3)
+            st2 = st2_tiles[(g, h)][0]
+            part = st2[:, :, 256 * u : 256 * u + 256].rearrange("p c (e f) -> p c e f", e=2)
             if len(accs) == 1:
-                nc.scalar.copy(
-                    out=split_ef(st2[:]), in_=accs[0][:].rearrange("p e (c f) -> p c e f", c=2)
-                )
+                nc.scalar.copy(out=part, in_=accs[0][:].rearrange("p e (c f) -> p c e f", c=2))
             else:
                 for e in range(2):
-                    nc.scalar.copy(
-                        out=split_ef(st2[:])[:, :, e, :],
-                        in_=accs[e][:].rearrange("p (c f) -> p c f", c=2),
-                    )
-            nc.sync.dma_start(out=dram_rows(out_1, i, h), in_=split_ef(st2[:]))
-            return st2
-
-        def hop2_xt2(i, h, st2):
-            st3 = st3p.tile([P, 2, 256], F32, name="st3")
+                    nc.scalar.copy(out=part[:, :, e, :], in_=accs[e][:].rearrange("p (c f) -> p c f", c=2))
+            if STG == 1:
+                nc.sync.dma_start(out=dram_rows_w(out_1, i, h), in_=st2[:, :, 256 * u : 256 * u + 256])
+            elif u == 1:
+                nc.sync.dma_start(out=dram_rows(out_1, g, h), in_=st2[:])
+        def hop2_xt2(i, h):
+            g, u = divmod(i, 2)
+            st2, st3 = st2_tiles[(g, h)]
+            cs = slice(256 * u, 256 * u + 256)
             nc.vector.scalar_tensor_tensor(
-                out=st3[:],
-                in0=st2[:],
-                scalar=2.0,
-                in1=xraw[:, 2 * h : 2 * h + 2, 256 * i : 256 * i + 256],
-                op0=MULT,
-                op1=SUB,
+                out=st3[:, :, cs], in0=st2[:, :, cs], scalar=2.0,
+                in1=xraw[:, 2 * h : 2 * h + 2, 256 * i : 256 * i + 256], op0=MULT, op1=SUB,
             )
-            nc.sync.dma_start(out=dram_rows(out_2, i, h), in_=split_ef(st3[:]))
-
-        transposes(0, ())
-        warm(0, 4)
-        warm(1, 5)
+            if STG == 1:
+                nc.sync.dma_start(out=dram_rows_w(out_2, i, h), in_=st3[:, :, cs])
+            elif u == 1:
+                nc.sync.dma_start(out=dram_rows(out_2, g, h), in_=st3[:])
+        rot = [0]
+        def abank():
+            k = 4 + rot[0] % 4
+            rot[0] += 1
+            return k
+        for e in range(2): transposes(0, e)
+        for r in range(WARM):
+            w = bank(4 + r % 4, [P, 512])
+            nc.tensor.matmul(out=w[:], lhsT=xraw[:, r % 2, 0:P], rhs=xraw[:, r % 2, 0:512], start=True, stop=True)
         x_regroup(0)
-        l_quant(0)
+        l_quant(0, 0); l_quant(0, 1)
         x_regroup(1)
         x_quant(0)
+        h1 = []
+        def m1(j):
+            acc = bank(abank(), [P, 2, 256])
+            for e in range(2): passes_e(acc, j, e, 1, xqc, xqs)
+            hop1_out(j, 1, acc)
         for i in range(NI):
-            if i + 1 < NI:
-                transposes(i + 1, (1, 3) if i + 1 == NI - 1 else (1,))
-            acc = passes(4 + i % 4, i, 0, xqc, xqs)
-            if i == NI - 2:
-                l_quant(i + 1)
-                hop1_quant(i // 2 - 1, 0)
+            if i == 2 and LAG < 99:
+                x_regroup(2)
+            acc = bank(abank(), [P, 2, 256])
+            if SPLIT:
+                for e in range(2):
+                    if i + 1 < NI: transposes(i + 1, e)
+                    passes_e(acc, i, e, 0, xqc, xqs)
             else:
-                if i % 2 == 0 and i > 0:
-                    hop1_quant(i // 2 - 1, 0)
                 if i + 1 < NI:
-                    l_quant(i + 1)
+                    for e in range(2): transposes(i + 1, e)
+                for e in range(2): passes_e(acc, i, e, 0, xqc, xqs)
             hop1_out(i, 0, acc)
-
-        n_open = 3
+            if i == 2 and LAG < 99:
+                x_regroup(3)
+            if i % 2 == 0 and i > 0: hop1_quant(i // 2 - 1, 0)
+            if i + 1 < NI:
+                l_quant(i + 1, 0); l_quant(i + 1, 1)
+            if i == 2 and LAG < 99:
+                x_quant(1)
+            j = i - LAG
+            if j >= 0:
+                m1(j); h1.append(j)
+                if j % 2 == 1: hop1_quant(j // 2, 1)
         opened = {}
-        for j in range(n_open):
+        for j in range(NOPEN):
             opened[j] = []
             for e in range(2):
                 acc = bank(2 * j + e, [P, 256])
-                for g in range(NG - 1):
-                    one_pass(acc[:], j, e, g, 0, yqc, yqs)
+                for g in range(NG - 1): one_pass(acc[:], j, e, g, 0, yqc, yqs)
                 opened[j].append(acc)
         hop1_quant(3, 0)
-        x_regroup(2)
-        st2_open = {}
-        for j in range(n_open):
-            for e in range(2):
-                one_pass(opened[j][e][:], j, e, NG - 1, 0, yqc, yqs)
-            st2_open[j] = hop2_x2(j, 0, opened[j])
-        x_regroup(3)
-        x_quant(1)
-        for j in range(n_open):
-            hop2_xt2(j, 0, st2_open[j])
-
-        rot = [2 * n_open]
-
+        if LAG == 99: x_regroup(2)
+        for j in range(NOPEN):
+            for e in range(2): one_pass(opened[j][e][:], j, e, NG - 1, 0, yqc, yqs)
+            hop2_x2(j, 0, opened[j])
+        if LAG == 99:
+            x_regroup(3)
+            x_quant(1)
+        for j in range(NOPEN): hop2_xt2(j, 0)
+        rot2 = [2 * NOPEN]
         def next_bank():
-            k = rot[0] % 8
-            rot[0] += 1
+            k = rot2[0] % 8
+            rot2[0] += 1
             return k
-
         def hop1_b(i):
-            acc = passes(next_bank(), i, 1, xqc, xqs)
+            acc = bank(next_bank(), [P, 2, 256])
+            for e in range(2): passes_e(acc, i, e, 1, xqc, xqs)
             hop1_out(i, 1, acc)
-            if i % 2 == 1:
-                hop1_quant(i // 2, 1)
-
+            if i % 2 == 1: hop1_quant(i // 2, 1)
         def hop2(i, h):
-            acc = passes(next_bank(), i, h, yqc, yqs)
-            st2 = hop2_x2(i, h, [acc])
-            hop2_xt2(i, h, st2)
-
-        hop2(3, 0)
-        hop2(4, 0)
-        for i in range(NI):
-            hop1_b(i)
-            if i == NI - 2:
-                hop2(5, 0)
-        hop2(6, 0)
-        hop2(7, 0)
-
-        for j in range(NI):
-            hop2(j, 1)
+            acc = bank(next_bank(), [P, 2, 256])
+            for e in range(2): passes_e(acc, i, e, h, yqc, yqs)
+            hop2_x2(i, h, [acc])
+            hop2_xt2(i, h)
+        if BSEQ:
+            for k, n in BSEQ:
+                if k == 'a': hop1_b(n)
+                elif k == 'b': hop2(n, 0)
+                else: hop2(n, 1)
+        else:
+            rest = [j for j in range(NI) if j not in h1]
+            two = [j for j in range(NOPEN, NI)]
+            a = two[:2]; two = two[2:]
+            for j in a: hop2(j, 0)
+            for n, j in enumerate(rest):
+                hop1_b(j)
+                if n == len(rest) - 2 and two: hop2(two.pop(0), 0)
+            for j in two: hop2(j, 0)
+            for j in range(NI): hop2(j, 1)

@@ -14,7 +14,8 @@ NI = N // 256
 NG = N // 512
 FLOPS = 2 * 2 * N * N * B * F
 SPLIT=False
-VEV=[1]
+DEINT=[2,4,6]
+VEV=[9]
 LAG=99
 NOPEN=3
 XORDER=[["l",0],["x",0],["x",1],["l",1],["l",2],["l",3],["l",4],["l",5],["l",6],["l",7],["x",2],["x",3]]
@@ -28,6 +29,7 @@ def tile_gcncheb_pa_kernel(tc, x, L, out_0, out_1, out_2):
         ctx.enter_context(tc.manual_schedule())
         keep = ctx.enter_context(tc.tile_pool(name="keep", bufs=1))
         lgp = ctx.enter_context(tc.tile_pool(name="lgp", bufs=4))
+        ldp = ctx.enter_context(tc.tile_pool(name="ldp", bufs=1))
         xgp = ctx.enter_context(tc.tile_pool(name="xgp", bufs=2))
         x1gp = ctx.enter_context(tc.tile_pool(name="x1gp", bufs=2))
         st1p = ctx.enter_context(tc.tile_pool(name="st1p", bufs=4))
@@ -79,6 +81,12 @@ def tile_gcncheb_pa_kernel(tc, x, L, out_0, out_1, out_2):
                 in_=xg_tiles[h][:].rearrange("p g c f t -> p (g c f t)"),
             )
         lg_tiles = {}
+        ld_tiles = {}
+        def deint(i):
+            for e in range(2):
+                ld = ldp.tile([P, 2, 512], F32, name="ld%d" % e)
+                ld_tiles[(i, e)] = ld
+                nc.vector.tensor_copy(out=ld[:], in_=lraw[i][:, e, :].bitcast(F32).rearrange("p (w u) -> p u w", u=2))
         def transposes(i, e):
             lw = lraw[i][:, e, :].bitcast(F32)
             lg = lgp.tile([P, N], BF16, name="lg", align_bytes=64)
@@ -87,8 +95,12 @@ def tile_gcncheb_pa_kernel(tc, x, L, out_0, out_1, out_2):
             for gg in range(2):
                 tp = bank(2 * e + gg, [P, 4, P])
                 for s in range(4):
-                    w0 = 512 * gg + 256 * (s // 2)
-                    src1 = lw[:, w0 + s % 2 : w0 + 256 : 2]
+                    if i in DEINT:
+                        g = 2 * gg + s // 2
+                        src1 = ld_tiles[(i, e)][:, s % 2, P * g : P * g + P]
+                    else:
+                        w0 = 512 * gg + 256 * (s // 2)
+                        src1 = lw[:, w0 + s % 2 : w0 + 256 : 2]
                     nc.tensor.transpose(tp[:, s, :], src1, ident[:])
                 src = tp[:].rearrange("p (g u) c -> p g c u", u=2)
                 dst = lgw[:, 2 * gg : 2 * gg + 2, :, :]
@@ -179,6 +191,7 @@ def tile_gcncheb_pa_kernel(tc, x, L, out_0, out_1, out_2):
             k = 4 + rot[0] % 4
             rot[0] += 1
             return k
+        if 0 in DEINT: deint(0)
         for e in range(2): transposes(0, e)
         for r in range(WARM):
             w = bank(4 + r % 4, [P, 512])
@@ -187,6 +200,7 @@ def tile_gcncheb_pa_kernel(tc, x, L, out_0, out_1, out_2):
         l_quant(0, 0); l_quant(0, 1)
         x_regroup(1)
         x_quant(0)
+        if 1 in DEINT: deint(1)
         h1 = []
         def m1(j):
             acc = bank(abank(), [P, 2, 256])
@@ -205,6 +219,7 @@ def tile_gcncheb_pa_kernel(tc, x, L, out_0, out_1, out_2):
                     for e in range(2): transposes(i + 1, e)
                 for e in range(2): passes_e(acc, i, e, 0, xqc, xqs)
             hop1_out(i, 0, acc)
+            if i + 2 < NI and i + 2 in DEINT: deint(i + 2)
             if i == 2 and LAG < 99:
                 x_regroup(3)
             if i % 2 == 0 and i > 0: hop1_quant(i // 2 - 1, 0)

@@ -1,6 +1,8 @@
 from contextlib import ExitStack
+
 import concourse.mybir as mybir
 from concourse.masks import make_identity
+
 F32 = mybir.dt.float32
 BF16 = mybir.dt.bfloat16
 U32 = mybir.dt.uint32
@@ -8,20 +10,15 @@ U8 = mybir.dt.uint8
 FP8X4 = mybir.dt.float8_e4m3fn_x4
 MULT = mybir.AluOpType.mult
 SUB = mybir.AluOpType.subtract
+
 P = 128
 B, N, F = 4, 2048, 128
 NI = N // 256
 NG = N // 512
 FLOPS = 2 * 2 * N * N * B * F
-SPLIT=False
-DEINT=[2,4,6]
-VEV=[9]
-LAG=99
-NOPEN=3
-XORDER=[["l",0],["x",0],["x",1],["l",1],["l",2],["l",3],["l",4],["l",5],["l",6],["l",7],["x",2],["x",3]]
-STG=2
-WARM=6
-BSEQ=[["b",3],["b",4],["b",5],["b",6],["a",0],["a",1],["a",2],["a",3],["a",4],["a",5],["a",6],["a",7],["b",7],["c",0],["c",1],["c",2],["c",3],["c",4],["c",5],["c",6],["c",7]]
+REORDERED = (2, 3, 4, 5, 6)
+HALVED = (0, 1)
+
 
 def tile_gcncheb_pa_kernel(tc, x, L, out_0, out_1, out_2):
     nc = tc.nc
@@ -29,17 +26,20 @@ def tile_gcncheb_pa_kernel(tc, x, L, out_0, out_1, out_2):
         ctx.enter_context(tc.manual_schedule())
         keep = ctx.enter_context(tc.tile_pool(name="keep", bufs=1))
         lgp = ctx.enter_context(tc.tile_pool(name="lgp", bufs=4))
-        ldp = ctx.enter_context(tc.tile_pool(name="ldp", bufs=1))
-        xgp = ctx.enter_context(tc.tile_pool(name="xgp", bufs=2))
+        ldp = ctx.enter_context(tc.tile_pool(name="ldp", bufs=4))
+        xgp = ctx.enter_context(tc.tile_pool(name="xgp", bufs=1))
         x1gp = ctx.enter_context(tc.tile_pool(name="x1gp", bufs=2))
         st1p = ctx.enter_context(tc.tile_pool(name="st1p", bufs=4))
         st2p = ctx.enter_context(tc.tile_pool(name="st2p", bufs=4))
         st3p = ctx.enter_context(tc.tile_pool(name="st3p", bufs=4))
         psum = ctx.enter_context(tc.psum_pool(name="psum", bufs=1))
+
         def bank(k, shape):
             return psum.tile(shape, F32, name="bank%d" % k, tag="bank%d" % k)
+
         ident = keep.tile([P, P], F32, name="ident")
         make_identity(nc, ident[:])
+
         lraw = [keep.tile([P, 2, N], BF16, name="lraw%d" % i) for i in range(NI)]
         xraw = keep.tile([P, B, N], BF16, name="xraw")
         ltc = keep.tile([P, NI, 2, 512], U32, name="ltc", align_bytes=64)
@@ -49,22 +49,31 @@ def tile_gcncheb_pa_kernel(tc, x, L, out_0, out_1, out_2):
         yqc = keep.tile([P, 2, NG, 256], U32, name="yqc", align_bytes=64)
         yqs = keep.tile([P, 2, NG, 256], U8, name="yqs", align_bytes=64)
 
-        def lview(i):
-            return L[512 * (i // 2) : 512 * (i // 2) + 512, :].rearrange("(p w e) b -> p w e b", w=2, e=2)[:, i % 2]
         def load_l(i):
-            nc.sync.dma_start(out=lraw[i][:], in_=lview(i))
-        def load_lh(i, e):
-            nc.sync.dma_start(out=lraw[i][:, e], in_=lview(i)[:, e])
+            g0 = 512 * (i // 2)
+            rows = L[g0 : g0 + 512, :].rearrange("(p w e) b -> p w e b", w=2, e=2)[:, i % 2]
+            if i in HALVED:
+                for e in range(2):
+                    nc.sync.dma_start(out=lraw[i][:, e], in_=rows[:, e])
+            else:
+                nc.sync.dma_start(out=lraw[i][:], in_=rows)
+
         def load_x(c):
             nc.sync.dma_start(
                 out=xraw[:, c, :].rearrange("p (g t f) -> p g t f", t=4, f=F),
                 in_=x[c].rearrange("(g p t) f -> p g t f", p=P, t=4),
             )
-        for k, n in XORDER:
-            if k == 'l': load_l(n)
-            elif k == 'x': load_x(n)
-            elif k == 'h': load_lh(n // 2, n % 2)
+
+        load_l(0)
+        load_x(0)
+        load_x(1)
+        for i in range(1, NI):
+            load_l(i)
+        load_x(2)
+        load_x(3)
+
         xg_tiles = {}
+
         def x_regroup(c):
             h, c2 = divmod(c, 2)
             if c2 == 0:
@@ -74,42 +83,55 @@ def tile_gcncheb_pa_kernel(tc, x, L, out_0, out_1, out_2):
                 out=xg_tiles[h][:, :, c2, :, :],
                 in_=xraw[:, c, :].rearrange("p (g t f) -> p g f t", t=4, f=F),
             )
+
         def x_quant(h):
             nc.vector.quantize_mx(
                 out=xqc[:, h].rearrange("p g w -> p (g w)").bitcast(FP8X4),
                 scales=xqs[:, h].rearrange("p g w -> p (g w)"),
                 in_=xg_tiles[h][:].rearrange("p g c f t -> p (g c f t)"),
             )
-        lg_tiles = {}
+
         ld_tiles = {}
-        def deint(i):
+
+        def reorder(i):
             for e in range(2):
-                ld = ldp.tile([P, 2, 512], F32, name="ld%d" % e)
+                ld = ldp.tile([P, 2, 512], F32, name="ld")
                 ld_tiles[(i, e)] = ld
-                nc.vector.tensor_copy(out=ld[:], in_=lraw[i][:, e, :].bitcast(F32).rearrange("p (w u) -> p u w", u=2))
-        def transposes(i, e):
-            lw = lraw[i][:, e, :].bitcast(F32)
-            lg = lgp.tile([P, N], BF16, name="lg", align_bytes=64)
-            lg_tiles[(i, e)] = lg
-            lgw = lg[:].bitcast(F32).rearrange("p (g c u) -> p g c u", c=P, u=2)
-            for gg in range(2):
-                tp = bank(2 * e + gg, [P, 4, P])
-                for s in range(4):
-                    if i in DEINT:
-                        g = 2 * gg + s // 2
-                        src1 = ld_tiles[(i, e)][:, s % 2, P * g : P * g + P]
-                    else:
-                        w0 = 512 * gg + 256 * (s // 2)
-                        src1 = lw[:, w0 + s % 2 : w0 + 256 : 2]
-                    nc.tensor.transpose(tp[:, s, :], src1, ident[:])
-                src = tp[:].rearrange("p (g u) c -> p g c u", u=2)
-                dst = lgw[:, 2 * gg : 2 * gg + 2, :, :]
-                if 2 * e + gg in VEV[i % len(VEV)] if isinstance(VEV[0], list) else 2 * e + gg in VEV:
-                    nc.vector.tensor_copy(out=dst, in_=src)
-                else:
-                    nc.scalar.copy(out=dst, in_=src)
-        def l_quant(i, e):
-            nc.vector.quantize_mx(out=ltc[:, i, e, :].bitcast(FP8X4), scales=lts[:, i, e, :], in_=lg_tiles[(i, e)][:])
+                nc.vector.tensor_copy(
+                    out=ld[:],
+                    in_=lraw[i][:, e, :].bitcast(F32).rearrange("p (w u) -> p u w", u=2),
+                )
+
+        lg_tiles = {}
+
+        def transposes(i):
+            for e in range(2):
+                lw = lraw[i][:, e, :].bitcast(F32)
+                lg = lgp.tile([P, N], BF16, name="lg", align_bytes=64)
+                lg_tiles[(i, e)] = lg
+                lgw = lg[:].bitcast(F32).rearrange("p (g c u) -> p g c u", c=P, u=2)
+                for gg in range(2):
+                    tp = bank(2 * e + gg, [P, 4, P])
+                    for s in range(4):
+                        g, u = 2 * gg + s // 2, s % 2
+                        if i in REORDERED:
+                            words = ld_tiles[(i, e)][:, u, P * g : P * g + P]
+                        else:
+                            words = lw[:, 256 * g + u : 256 * g + 256 : 2]
+                        nc.tensor.transpose(tp[:, s, :], words, ident[:])
+                    nc.scalar.copy(
+                        out=lgw[:, 2 * gg : 2 * gg + 2, :, :],
+                        in_=tp[:].rearrange("p (g u) c -> p g c u", u=2),
+                    )
+
+        def l_quant(i):
+            for e in range(2):
+                nc.vector.quantize_mx(
+                    out=ltc[:, i, e, :].bitcast(FP8X4),
+                    scales=lts[:, i, e, :],
+                    in_=lg_tiles[(i, e)][:],
+                )
+
         def one_pass(out, i, e, g, h, rc, rs):
             nc.tensor.matmul_mx(
                 out=out,
@@ -120,160 +142,162 @@ def tile_gcncheb_pa_kernel(tc, x, L, out_0, out_1, out_2):
                 start=(g == 0),
                 stop=(g == NG - 1),
             )
-        def passes_e(acc, i, e, h, rc, rs):
-            for g in range(NG):
-                one_pass(acc[:, e, :], i, e, g, h, rc, rs)
+
+        def passes(k, i, h, rc, rs):
+            acc = bank(k, [P, 2, 256])
+            for e in range(2):
+                for g in range(NG):
+                    one_pass(acc[:, e, :], i, e, g, h, rc, rs)
+            return acc
+
         def dram_rows(o, g, h):
-            return o[2 * h : 2 * h + 2, 512 * g : 512 * g + 512, :].rearrange("c (p t) f -> p c (t f)", t=4)
-        def dram_rows_c(o, g, c):
-            return o[c, 512 * g : 512 * g + 512, :].rearrange("(p t) f -> p (t f)", t=4)
-        def dram_rows_w(o, i, h):
-            g0 = 512 * (i // 2)
-            return o[2 * h : 2 * h + 2, g0 : g0 + 512, :].rearrange("c (p w e) f -> p c w (e f)", w=2, e=2)[:, :, i % 2]
+            return o[2 * h : 2 * h + 2, 512 * g : 512 * g + 512, :].rearrange(
+                "c (p t) f -> p c (t f)", t=4
+            )
+
+        def tile_part(s, i):
+            return s[:, :, 256 * (i % 2) : 256 * (i % 2) + 256]
+
+        def empty(s, i, acc):
+            nc.scalar.copy(
+                out=tile_part(s, i).rearrange("p c (e f) -> p c e f", f=F),
+                in_=acc[:].rearrange("p e (c f) -> p c e f", f=F),
+            )
+
         st1_tiles = {}
-        def hop1_out(i, h, acc):
-            gq, u = divmod(i, 2)
-            if u == 0:
+
+        def hop1(k, i, h):
+            acc = passes(k, i, h, xqc, xqs)
+            g, w = divmod(i, 2)
+            if w == 0:
                 st1 = st1p.tile([P, 2, 512], F32, name="st1")
-                st1_tiles[(gq, h)] = st1
-            part = st1_tiles[(gq, h)][:, :, 256 * u : 256 * u + 256].rearrange("p c (e f) -> p c e f", e=2)
-            nc.scalar.copy(out=part, in_=acc[:].rearrange("p e (c f) -> p c e f", c=2))
-            if STG == 1:
-                nc.sync.dma_start(out=dram_rows_w(out_0, i, h), in_=st1_tiles[(gq, h)][:, :, 256 * u : 256 * u + 256])
-            elif u == 1:
-                nc.sync.dma_start(out=dram_rows(out_0, gq, h), in_=st1_tiles[(gq, h)][:])
+                st1_tiles[(g, h)] = st1
+            empty(st1_tiles[(g, h)], i, acc)
+            if w == 1:
+                nc.sync.dma_start(out=dram_rows(out_0, g, h), in_=st1_tiles[(g, h)][:])
+
         x1g_tiles = {}
-        def hop1_regroup(gq, h):
+
+        def x1_regroup(g, h):
             x1g = x1gp.tile([P, 2, F, 4], BF16, name="x1g", align_bytes=64)
-            x1g_tiles[(gq, h)] = x1g
-            nc.vector.tensor_copy(out=x1g[:], in_=st1_tiles[(gq, h)][:].rearrange("p c (t f) -> p c f t", t=4))
-        def hop1_q(gq, h):
+            x1g_tiles[(g, h)] = x1g
+            nc.vector.tensor_copy(
+                out=x1g[:],
+                in_=st1_tiles[(g, h)][:].rearrange("p c (t f) -> p c f t", t=4),
+            )
+
+        def x1_quant(g, h):
             nc.vector.quantize_mx(
-                out=yqc[:, h, gq, :].bitcast(FP8X4),
-                scales=yqs[:, h, gq, :],
-                in_=x1g_tiles[(gq, h)][:].rearrange("p c f t -> p (c f t)"),
+                out=yqc[:, h, g, :].bitcast(FP8X4),
+                scales=yqs[:, h, g, :],
+                in_=x1g_tiles[(g, h)][:].rearrange("p c f t -> p (c f t)"),
             )
-        def hop1_quant(gq, h):
-            hop1_regroup(gq, h)
-            hop1_q(gq, h)
+
         st2_tiles = {}
-        def hop2_x2(i, h, accs):
-            g, u = divmod(i, 2)
-            if u == 0:
-                st2 = st2p.tile([P, 2, 512], F32, name="st2")
-                st3 = st3p.tile([P, 2, 512], F32, name="st3")
-                st2_tiles[(g, h)] = (st2, st3)
-            st2 = st2_tiles[(g, h)][0]
-            part = st2[:, :, 256 * u : 256 * u + 256].rearrange("p c (e f) -> p c e f", e=2)
-            if len(accs) == 1:
-                nc.scalar.copy(out=part, in_=accs[0][:].rearrange("p e (c f) -> p c e f", c=2))
-            else:
-                for e in range(2):
-                    nc.scalar.copy(out=part[:, :, e, :], in_=accs[e][:].rearrange("p (c f) -> p c f", c=2))
-            if STG == 1:
-                nc.sync.dma_start(out=dram_rows_w(out_1, i, h), in_=st2[:, :, 256 * u : 256 * u + 256])
-            elif u == 1:
-                nc.sync.dma_start(out=dram_rows(out_1, g, h), in_=st2[:])
-        def hop2_xt2(i, h):
-            g, u = divmod(i, 2)
-            st2, st3 = st2_tiles[(g, h)]
-            cs = slice(256 * u, 256 * u + 256)
+        st3_tiles = {}
+
+        def stage2(g, h):
+            st2 = st2p.tile([P, 2, 512], F32, name="st2")
+            st3 = st3p.tile([P, 2, 512], F32, name="st3")
+            st2_tiles[(g, h)] = st2
+            st3_tiles[(g, h)] = st3
+
+        def xt2(i, h):
+            g, w = divmod(i, 2)
             nc.vector.scalar_tensor_tensor(
-                out=st3[:, :, cs], in0=st2[:, :, cs], scalar=2.0,
-                in1=xraw[:, 2 * h : 2 * h + 2, 256 * i : 256 * i + 256], op0=MULT, op1=SUB,
+                out=tile_part(st3_tiles[(g, h)], i),
+                in0=tile_part(st2_tiles[(g, h)], i),
+                scalar=2.0,
+                in1=xraw[:, 2 * h : 2 * h + 2, 256 * i : 256 * i + 256],
+                op0=MULT,
+                op1=SUB,
             )
-            if STG == 1:
-                nc.sync.dma_start(out=dram_rows_w(out_2, i, h), in_=st3[:, :, cs])
-            elif u == 1:
-                nc.sync.dma_start(out=dram_rows(out_2, g, h), in_=st3[:])
-        rot = [0]
-        def abank():
-            k = 4 + rot[0] % 4
-            rot[0] += 1
-            return k
-        if 0 in DEINT: deint(0)
-        for e in range(2): transposes(0, e)
-        for r in range(WARM):
+
+        def store2(g, h, o, tiles):
+            nc.sync.dma_start(out=dram_rows(o, g, h), in_=tiles[(g, h)][:])
+
+        def hop2(k, i, h):
+            acc = passes(k, i, h, yqc, yqs)
+            g, w = divmod(i, 2)
+            if w == 0:
+                stage2(g, h)
+            empty(st2_tiles[(g, h)], i, acc)
+            if w == 1:
+                store2(g, h, out_1, st2_tiles)
+            xt2(i, h)
+            if w == 1:
+                store2(g, h, out_2, st3_tiles)
+
+        transposes(0)
+        for r in range(6):
             w = bank(4 + r % 4, [P, 512])
-            nc.tensor.matmul(out=w[:], lhsT=xraw[:, r % 2, 0:P], rhs=xraw[:, r % 2, 0:512], start=True, stop=True)
+            nc.tensor.matmul(
+                out=w[:], lhsT=xraw[:, 0, 0:P], rhs=xraw[:, 0, 0:512], start=True, stop=True
+            )
         x_regroup(0)
-        l_quant(0, 0); l_quant(0, 1)
+        l_quant(0)
         x_regroup(1)
         x_quant(0)
-        if 1 in DEINT: deint(1)
-        h1 = []
-        def m1(j):
-            acc = bank(abank(), [P, 2, 256])
-            for e in range(2): passes_e(acc, j, e, 1, xqc, xqs)
-            hop1_out(j, 1, acc)
         for i in range(NI):
-            if i == 2 and LAG < 99:
-                x_regroup(2)
-            acc = bank(abank(), [P, 2, 256])
-            if SPLIT:
-                for e in range(2):
-                    if i + 1 < NI: transposes(i + 1, e)
-                    passes_e(acc, i, e, 0, xqc, xqs)
-            else:
-                if i + 1 < NI:
-                    for e in range(2): transposes(i + 1, e)
-                for e in range(2): passes_e(acc, i, e, 0, xqc, xqs)
-            hop1_out(i, 0, acc)
-            if i + 2 < NI and i + 2 in DEINT: deint(i + 2)
-            if i == 2 and LAG < 99:
-                x_regroup(3)
-            if i % 2 == 0 and i > 0: hop1_quant(i // 2 - 1, 0)
             if i + 1 < NI:
-                l_quant(i + 1, 0); l_quant(i + 1, 1)
-            if i == 2 and LAG < 99:
-                x_quant(1)
-            j = i - LAG
-            if j >= 0:
-                m1(j); h1.append(j)
-                if j % 2 == 1: hop1_quant(j // 2, 1)
+                transposes(i + 1)
+            hop1(4 + i % 4, i, 0)
+            if i + 2 in REORDERED:
+                reorder(i + 2)
+            x1_ready = i // 2 - 1 if i % 2 == 0 and 0 < i else -1
+            if x1_ready >= 0:
+                x1_regroup(x1_ready, 0)
+            if i + 1 < NI:
+                l_quant(i + 1)
+            if x1_ready >= 0:
+                x1_quant(x1_ready, 0)
+
+        n_open = 3
         opened = {}
-        for j in range(NOPEN):
-            opened[j] = []
+        for j in range(n_open):
             for e in range(2):
                 acc = bank(2 * j + e, [P, 256])
-                for g in range(NG - 1): one_pass(acc[:], j, e, g, 0, yqc, yqs)
-                opened[j].append(acc)
-        hop1_quant(3, 0)
-        if LAG == 99: x_regroup(2)
-        for j in range(NOPEN):
-            for e in range(2): one_pass(opened[j][e][:], j, e, NG - 1, 0, yqc, yqs)
-            hop2_x2(j, 0, opened[j])
-        if LAG == 99:
-            x_regroup(3)
-            x_quant(1)
-        for j in range(NOPEN): hop2_xt2(j, 0)
-        rot2 = [2 * NOPEN]
+                opened[(j, e)] = acc
+                for g in range(NG - 1):
+                    one_pass(acc[:], j, e, g, 0, yqc, yqs)
+        x1_regroup(3, 0)
+        x1_quant(3, 0)
+        x_regroup(2)
+        x_regroup(3)
+        x_quant(1)
+        for j in range(n_open):
+            g, w = divmod(j, 2)
+            if w == 0:
+                stage2(g, 0)
+            for e in range(2):
+                one_pass(opened[(j, e)][:], j, e, NG - 1, 0, yqc, yqs)
+                nc.scalar.copy(
+                    out=tile_part(st2_tiles[(g, 0)], j)[:, :, F * e : F * e + F],
+                    in_=opened[(j, e)][:].rearrange("p (c f) -> p c f", f=F),
+                )
+            if w == 1:
+                store2(g, 0, out_1, st2_tiles)
+        for j in range(n_open):
+            xt2(j, 0)
+            if j % 2 == 1:
+                store2(j // 2, 0, out_2, st3_tiles)
+
+        used = [2 * n_open]
+
         def next_bank():
-            k = rot2[0] % 8
-            rot2[0] += 1
+            k = used[0] % 8
+            used[0] += 1
             return k
-        def hop1_b(i):
-            acc = bank(next_bank(), [P, 2, 256])
-            for e in range(2): passes_e(acc, i, e, 1, xqc, xqs)
-            hop1_out(i, 1, acc)
-            if i % 2 == 1: hop1_quant(i // 2, 1)
-        def hop2(i, h):
-            acc = bank(next_bank(), [P, 2, 256])
-            for e in range(2): passes_e(acc, i, e, h, yqc, yqs)
-            hop2_x2(i, h, [acc])
-            hop2_xt2(i, h)
-        if BSEQ:
-            for k, n in BSEQ:
-                if k == 'a': hop1_b(n)
-                elif k == 'b': hop2(n, 0)
-                else: hop2(n, 1)
-        else:
-            rest = [j for j in range(NI) if j not in h1]
-            two = [j for j in range(NOPEN, NI)]
-            a = two[:2]; two = two[2:]
-            for j in a: hop2(j, 0)
-            for n, j in enumerate(rest):
-                hop1_b(j)
-                if n == len(rest) - 2 and two: hop2(two.pop(0), 0)
-            for j in two: hop2(j, 0)
-            for j in range(NI): hop2(j, 1)
+
+        for j in range(n_open, 6):
+            hop2(next_bank(), j, 0)
+        for i in range(NI):
+            hop1(next_bank(), i, 1)
+            if i % 2 == 1:
+                x1_regroup(i // 2, 1)
+                x1_quant(i // 2, 1)
+        for j in range(6, NI):
+            hop2(next_bank(), j, 0)
+
+        for j in range(NI):
+            hop2(next_bank(), j, 1)

@@ -17,7 +17,7 @@ NI = N // 256
 NG = N // 512
 FLOPS = 2 * 2 * N * N * B * F
 REORDERED = (2, 3, 4, 5, 6)
-HALVED = (0, 1)
+HALVED = (0, 1, 2, 3)
 
 
 def tile_gcncheb_pa_kernel(tc, x, L, out_0, out_1, out_2):
@@ -79,10 +79,13 @@ def tile_gcncheb_pa_kernel(tc, x, L, out_0, out_1, out_2):
             if c2 == 0:
                 xg = xgp.tile([P, NG, 2, F, 4], BF16, name="xg", align_bytes=64)
                 xg_tiles[h] = xg
-            nc.vector.tensor_copy(
-                out=xg_tiles[h][:, :, c2, :, :],
-                in_=xraw[:, c, :].rearrange("p (g t f) -> p g f t", t=4, f=F),
-            )
+            src = xraw[:, c, :].rearrange("p (g t f) -> p g f t", t=4, f=F)
+            dst = xg_tiles[h][:, :, c2, :, :]
+            if c == 1:
+                nc.scalar.copy(out=dst[:, 2:4], in_=src[:, 2:4])
+                nc.vector.tensor_copy(out=dst[:, 0:2], in_=src[:, 0:2])
+            else:
+                nc.vector.tensor_copy(out=dst, in_=src)
 
         def x_quant(h):
             nc.vector.quantize_mx(
@@ -228,12 +231,15 @@ def tile_gcncheb_pa_kernel(tc, x, L, out_0, out_1, out_2):
             if w == 1:
                 store2(g, h, out_2, st3_tiles)
 
+        def warm(n):
+            for r in range(n):
+                w = bank(4 + r % 4, [P, 512])
+                nc.tensor.matmul(
+                    out=w[:], lhsT=xraw[:, 0, 0:P], rhs=xraw[:, 0, 0:512], start=True, stop=True
+                )
+
         transposes(0)
-        for r in range(6):
-            w = bank(4 + r % 4, [P, 512])
-            nc.tensor.matmul(
-                out=w[:], lhsT=xraw[:, 0, 0:P], rhs=xraw[:, 0, 0:512], start=True, stop=True
-            )
+        warm(6)
         x_regroup(0)
         l_quant(0)
         x_regroup(1)
@@ -241,6 +247,8 @@ def tile_gcncheb_pa_kernel(tc, x, L, out_0, out_1, out_2):
         for i in range(NI):
             if i + 1 < NI:
                 transposes(i + 1)
+            if i == 0:
+                warm(2)
             hop1(4 + i % 4, i, 0)
             if i + 2 in REORDERED:
                 reorder(i + 2)

@@ -217,7 +217,8 @@ def tile_gcncheb_pa_kernel(tc, x, L, out_0, out_1, out_2):
             )
 
         def store2(g, h, o, tiles):
-            nc.sync.dma_start(out=dram_rows(o, g, h), in_=tiles[(g, h)][:])
+            queue = nc.scalar if tiles is st2_tiles else nc.sync
+            queue.dma_start(out=dram_rows(o, g, h), in_=tiles[(g, h)][:])
 
         def hop2(k, i, h):
             acc = passes(k, i, h, yqc, yqs)

@@ -37,17 +37,17 @@ def tile_gcncheb_pa_kernel(tc, x, L, out_0, out_1, out_2):
         def bank(k, shape):
             return psum.tile(shape, F32, name="bank%d" % k, tag="bank%d" % k)
 
-        ident = keep.tile([P, P], F32, name="ident")
+        ident = keep.tile([P, P], F32, name="ident", align_bytes=256)
         make_identity(nc, ident[:])
 
-        lraw = [keep.tile([P, 2, N], BF16, name="lraw%d" % i) for i in range(NI)]
-        xraw = keep.tile([P, B, N], BF16, name="xraw")
-        ltc = keep.tile([P, NI, 2, 512], U32, name="ltc", align_bytes=64)
-        lts = keep.tile([P, NI, 2, 512], U8, name="lts", align_bytes=64)
-        xqc = keep.tile([P, 2, NG, 256], U32, name="xqc", align_bytes=64)
-        xqs = keep.tile([P, 2, NG, 256], U8, name="xqs", align_bytes=64)
-        yqc = keep.tile([P, 2, NG, 256], U32, name="yqc", align_bytes=64)
-        yqs = keep.tile([P, 2, NG, 256], U8, name="yqs", align_bytes=64)
+        lraw = [keep.tile([P, 2, N], BF16, name="lraw%d" % i, align_bytes=256) for i in range(NI)]
+        xraw = keep.tile([P, B, N], BF16, name="xraw", align_bytes=256)
+        ltc = keep.tile([P, NI, 2, 512], U32, name="ltc", align_bytes=256)
+        lts = keep.tile([P, NI, 2, 512], U8, name="lts", align_bytes=256)
+        xqc = keep.tile([P, 2, NG, 256], U32, name="xqc", align_bytes=256)
+        xqs = keep.tile([P, 2, NG, 256], U8, name="xqs", align_bytes=256)
+        yqc = keep.tile([P, 2, NG, 256], U32, name="yqc", align_bytes=256)
+        yqs = keep.tile([P, 2, NG, 256], U8, name="yqs", align_bytes=256)
 
         def load_l(i):
             g0 = 512 * (i // 2)
@@ -77,7 +77,7 @@ def tile_gcncheb_pa_kernel(tc, x, L, out_0, out_1, out_2):
         def x_regroup(c):
             h, c2 = divmod(c, 2)
             if c2 == 0:
-                xg = xgp.tile([P, NG, 2, F, 4], BF16, name="xg", align_bytes=64)
+                xg = xgp.tile([P, NG, 2, F, 4], BF16, name="xg", align_bytes=256)
                 xg_tiles[h] = xg
             src = xraw[:, c, :].rearrange("p (g t f) -> p g f t", t=4, f=F)
             dst = xg_tiles[h][:, :, c2, :, :]
@@ -98,7 +98,7 @@ def tile_gcncheb_pa_kernel(tc, x, L, out_0, out_1, out_2):
 
         def reorder(i):
             for e in range(2):
-                ld = ldp.tile([P, 2, 512], F32, name="ld")
+                ld = ldp.tile([P, 2, 512], F32, name="ld", align_bytes=256)
                 ld_tiles[(i, e)] = ld
                 nc.vector.tensor_copy(
                     out=ld[:],
@@ -110,7 +110,7 @@ def tile_gcncheb_pa_kernel(tc, x, L, out_0, out_1, out_2):
         def transposes(i):
             for e in range(2):
                 lw = lraw[i][:, e, :].bitcast(F32)
-                lg = lgp.tile([P, N], BF16, name="lg", align_bytes=64)
+                lg = lgp.tile([P, N], BF16, name="lg", align_bytes=256)
                 lg_tiles[(i, e)] = lg
                 lgw = lg[:].bitcast(F32).rearrange("p (g c u) -> p g c u", c=P, u=2)
                 for gg in range(2):
@@ -182,7 +182,7 @@ def tile_gcncheb_pa_kernel(tc, x, L, out_0, out_1, out_2):
         x1g_tiles = {}
 
         def x1_regroup(g, h):
-            x1g = x1gp.tile([P, 2, F, 4], BF16, name="x1g", align_bytes=64)
+            x1g = x1gp.tile([P, 2, F, 4], BF16, name="x1g", align_bytes=256)
             x1g_tiles[(g, h)] = x1g
             nc.vector.tensor_copy(
                 out=x1g[:],

@@ -81,7 +81,7 @@ def tile_gcncheb_pa_kernel(tc, x, L, out_0, out_1, out_2):
                 xg_tiles[h] = xg
             src = xraw[:, c, :].rearrange("p (g t f) -> p g f t", t=4, f=F)
             dst = xg_tiles[h][:, :, c2, :, :]
-            if c == 1:
+            if c % 2 == 1:
                 nc.scalar.copy(out=dst[:, 2:4], in_=src[:, 2:4])
                 nc.vector.tensor_copy(out=dst[:, 0:2], in_=src[:, 0:2])
             else:
@@ -122,10 +122,12 @@ def tile_gcncheb_pa_kernel(tc, x, L, out_0, out_1, out_2):
                         else:
                             words = lw[:, 256 * g + u : 256 * g + 256 : 2]
                         nc.tensor.transpose(tp[:, s, :], words, ident[:])
-                    nc.scalar.copy(
-                        out=lgw[:, 2 * gg : 2 * gg + 2, :, :],
-                        in_=tp[:].rearrange("p (g u) c -> p g c u", u=2),
-                    )
+                    src = tp[:].rearrange("p (g u) c -> p g c u", u=2)
+                    dst = lgw[:, 2 * gg : 2 * gg + 2, :, :]
+                    if i == NI - 1 and e == 0 and gg == 1:
+                        nc.vector.tensor_copy(out=dst, in_=src)
+                    else:
+                        nc.scalar.copy(out=dst, in_=src)
 
         def l_quant(i):
             for e in range(2):
@@ -173,7 +175,7 @@ def tile_gcncheb_pa_kernel(tc, x, L, out_0, out_1, out_2):
             acc = passes(k, i, h, xqc, xqs)
             g, w = divmod(i, 2)
             if w == 0:
-                st1 = st1p.tile([P, 2, 512], F32, name="st1")
+                st1 = st1p.tile([P, 2, 512], F32, name="st1", align_bytes=256)
                 st1_tiles[(g, h)] = st1
             empty(st1_tiles[(g, h)], i, acc)
             if w == 1:
@@ -200,8 +202,8 @@ def tile_gcncheb_pa_kernel(tc, x, L, out_0, out_1, out_2):
         st3_tiles = {}
 
         def stage2(g, h):
-            st2 = st2p.tile([P, 2, 512], F32, name="st2")
-            st3 = st3p.tile([P, 2, 512], F32, name="st3")
+            st2 = st2p.tile([P, 2, 512], F32, name="st2", align_bytes=256)
+            st3 = st3p.tile([P, 2, 512], F32, name="st3", align_bytes=256)
             st2_tiles[(g, h)] = st2
             st3_tiles[(g, h)] = st3
 
@@ -239,6 +241,39 @@ def tile_gcncheb_pa_kernel(tc, x, L, out_0, out_1, out_2):
                     out=w[:], lhsT=xraw[:, 0, 0:P], rhs=xraw[:, 0, 0:512], start=True, stop=True
                 )
 
+        def hop2_item(k, g, h, c):
+            acc = bank(k, [P, 4, F])
+            for t in range(4):
+                i, e = 2 * g + t // 2, t % 2
+                for gk in range(NG):
+                    nc.tensor.matmul_mx(
+                        out=acc[:, t, :],
+                        lhsT=ltc[:, i, e, P * gk : P * gk + P].bitcast(FP8X4),
+                        lhsT_scale=lts[:, i, e, P * gk : P * gk + P],
+                        rhs=yqc[:, h, gk, F * c : F * c + F].bitcast(FP8X4),
+                        rhs_scale=yqs[:, h, gk, F * c : F * c + F],
+                        start=(gk == 0),
+                        stop=(gk == NG - 1),
+                    )
+            if c == 0:
+                stage2(g, h)
+            st2 = st2_tiles[(g, h)][:, c, :]
+            st3 = st3_tiles[(g, h)][:, c, :]
+            nc.scalar.copy(out=st2, in_=acc[:].rearrange("p t f -> p (t f)"))
+            nc.scalar.dma_start(out=item_rows(out_1, g, 2 * h + c), in_=st2)
+            nc.vector.scalar_tensor_tensor(
+                out=st3,
+                in0=st2,
+                scalar=2.0,
+                in1=xraw[:, 2 * h + c, 512 * g : 512 * g + 512],
+                op0=MULT,
+                op1=SUB,
+            )
+            nc.sync.dma_start(out=item_rows(out_2, g, 2 * h + c), in_=st3)
+
+        def item_rows(o, g, c):
+            return o[c, 512 * g : 512 * g + 512, :].rearrange("(p t) f -> p (t f)", t=4)
+
         transposes(0)
         warm(6)
         x_regroup(0)
@@ -260,6 +295,8 @@ def tile_gcncheb_pa_kernel(tc, x, L, out_0, out_1, out_2):
                 l_quant(i + 1)
             if x1_ready >= 0:
                 x1_quant(x1_ready, 0)
+            if i == NI - 2:
+                x_regroup(2)
 
         n_open = 3
         opened = {}
@@ -271,9 +308,7 @@ def tile_gcncheb_pa_kernel(tc, x, L, out_0, out_1, out_2):
                     one_pass(acc[:], j, e, g, 0, yqc, yqs)
         x1_regroup(3, 0)
         x1_quant(3, 0)
-        x_regroup(2)
         x_regroup(3)
-        x_quant(1)
         for j in range(n_open):
             g, w = divmod(j, 2)
             if w == 0:
@@ -286,10 +321,11 @@ def tile_gcncheb_pa_kernel(tc, x, L, out_0, out_1, out_2):
                 )
             if w == 1:
                 store2(g, 0, out_1, st2_tiles)
-        for j in range(n_open):
-            xt2(j, 0)
-            if j % 2 == 1:
-                store2(j // 2, 0, out_2, st3_tiles)
+        xt2(0, 0)
+        xt2(1, 0)
+        store2(0, 0, out_2, st3_tiles)
+        x_quant(1)
+        xt2(2, 0)
 
         used = [2 * n_open]
 
@@ -305,8 +341,9 @@ def tile_gcncheb_pa_kernel(tc, x, L, out_0, out_1, out_2):
             if i % 2 == 1:
                 x1_regroup(i // 2, 1)
                 x1_quant(i // 2, 1)
-        for j in range(6, NI):
-            hop2(next_bank(), j, 0)
+        for c in range(2):
+            hop2_item(next_bank(), NG - 1, 0, c)
 
-        for j in range(NI):
-            hop2(next_bank(), j, 1)
+        for g in range(NG):
+            for c in range(2):
+                hop2_item(next_bank(), g, 1, c)

@@ -16,7 +16,7 @@ B, N, F = 4, 2048, 128
 NI = N // 256
 NG = N // 512
 FLOPS = 2 * 2 * N * N * B * F
-REORDERED = (2, 3, 4, 5, 6)
+RG = {2: 4, 3: 4, 4: 3, 5: 4, 6: 3}
 HALVED = (0, 1, 2, 3)
 
 
@@ -98,11 +98,11 @@ def tile_gcncheb_pa_kernel(tc, x, L, out_0, out_1, out_2):
 
         def reorder(i):
             for e in range(2):
-                ld = ldp.tile([P, 2, 512], F32, name="ld", align_bytes=256)
+                ld = ldp.tile([P, 2, P * RG[i]], F32, name="ld", align_bytes=256)
                 ld_tiles[(i, e)] = ld
                 nc.vector.tensor_copy(
                     out=ld[:],
-                    in_=lraw[i][:, e, :].bitcast(F32).rearrange("p (w u) -> p u w", u=2),
+                    in_=lraw[i][:, e, 0 : 512 * RG[i]].bitcast(F32).rearrange("p (w u) -> p u w", u=2),
                 )
 
         lg_tiles = {}
@@ -117,7 +117,7 @@ def tile_gcncheb_pa_kernel(tc, x, L, out_0, out_1, out_2):
                     tp = bank(2 * e + gg, [P, 4, P])
                     for s in range(4):
                         g, u = 2 * gg + s // 2, s % 2
-                        if i in REORDERED:
+                        if g < RG.get(i, 0):
                             words = ld_tiles[(i, e)][:, u, P * g : P * g + P]
                         else:
                             words = lw[:, 256 * g + u : 256 * g + 256 : 2]
@@ -241,39 +241,6 @@ def tile_gcncheb_pa_kernel(tc, x, L, out_0, out_1, out_2):
                     out=w[:], lhsT=xraw[:, 0, 0:P], rhs=xraw[:, 0, 0:512], start=True, stop=True
                 )
 
-        def hop2_item(k, g, h, c):
-            acc = bank(k, [P, 4, F])
-            for t in range(4):
-                i, e = 2 * g + t // 2, t % 2
-                for gk in range(NG):
-                    nc.tensor.matmul_mx(
-                        out=acc[:, t, :],
-                        lhsT=ltc[:, i, e, P * gk : P * gk + P].bitcast(FP8X4),
-                        lhsT_scale=lts[:, i, e, P * gk : P * gk + P],
-                        rhs=yqc[:, h, gk, F * c : F * c + F].bitcast(FP8X4),
-                        rhs_scale=yqs[:, h, gk, F * c : F * c + F],
-                        start=(gk == 0),
-                        stop=(gk == NG - 1),
-                    )
-            if c == 0:
-                stage2(g, h)
-            st2 = st2_tiles[(g, h)][:, c, :]
-            st3 = st3_tiles[(g, h)][:, c, :]
-            nc.scalar.copy(out=st2, in_=acc[:].rearrange("p t f -> p (t f)"))
-            nc.scalar.dma_start(out=item_rows(out_1, g, 2 * h + c), in_=st2)
-            nc.vector.scalar_tensor_tensor(
-                out=st3,
-                in0=st2,
-                scalar=2.0,
-                in1=xraw[:, 2 * h + c, 512 * g : 512 * g + 512],
-                op0=MULT,
-                op1=SUB,
-            )
-            nc.sync.dma_start(out=item_rows(out_2, g, 2 * h + c), in_=st3)
-
-        def item_rows(o, g, c):
-            return o[c, 512 * g : 512 * g + 512, :].rearrange("(p t) f -> p (t f)", t=4)
-
         transposes(0)
         warm(6)
         x_regroup(0)
@@ -283,10 +250,8 @@ def tile_gcncheb_pa_kernel(tc, x, L, out_0, out_1, out_2):
         for i in range(NI):
             if i + 1 < NI:
                 transposes(i + 1)
-            if i == 0:
-                warm(2)
             hop1(4 + i % 4, i, 0)
-            if i + 2 in REORDERED:
+            if i + 2 in RG:
                 reorder(i + 2)
             x1_ready = i // 2 - 1 if i % 2 == 0 and 0 < i else -1
             if x1_ready >= 0:
@@ -341,9 +306,8 @@ def tile_gcncheb_pa_kernel(tc, x, L, out_0, out_1, out_2):
             if i % 2 == 1:
                 x1_regroup(i // 2, 1)
                 x1_quant(i // 2, 1)
-        for c in range(2):
-            hop2_item(next_bank(), NG - 1, 0, c)
+        for j in range(6, NI):
+            hop2(next_bank(), j, 0)
 
-        for g in range(NG):
-            for c in range(2):
-                hop2_item(next_bank(), g, 1, c)
+        for j in range(NI):
+            hop2(next_bank(), j, 1)

@@ -79,8 +79,8 @@ def tile_gcncheb_pa_kernel(tc, x, L, out_0, out_1, out_2):
             if c2 == 0:
                 xg = xgp.tile([P, NG, 2, F, 4], BF16, name="xg", align_bytes=256)
                 xg_tiles[h] = xg
-            src = xraw[:, c, :].rearrange("p (g t f) -> p g f t", t=4, f=F)
-            dst = xg_tiles[h][:, :, c2, :, :]
+            src = xraw[:, c, :].rearrange("p (g t f i) -> p g f t i", t=4, f=F // 4, i=4)
+            dst = xg_tiles[h][:, :, c2, :, :].rearrange("p g (f i) t -> p g f t i", i=4)
             if c % 2 == 1:
                 nc.scalar.copy(out=dst[:, 2:4], in_=src[:, 2:4])
                 nc.vector.tensor_copy(out=dst[:, 0:2], in_=src[:, 0:2])
@@ -187,8 +187,8 @@ def tile_gcncheb_pa_kernel(tc, x, L, out_0, out_1, out_2):
             x1g = x1gp.tile([P, 2, F, 4], BF16, name="x1g", align_bytes=256)
             x1g_tiles[(g, h)] = x1g
             nc.vector.tensor_copy(
-                out=x1g[:],
-                in_=st1_tiles[(g, h)][:].rearrange("p c (t f) -> p c f t", t=4),
+                out=x1g[:].rearrange("p c (f i) t -> p c f t i", i=4),
+                in_=st1_tiles[(g, h)][:].rearrange("p c (t f i) -> p c f t i", t=4, i=4),
             )
 
         def x1_quant(g, h):

@@ -16,7 +16,7 @@ B, N, F = 4, 2048, 128
 NI = N // 256
 NG = N // 512
 FLOPS = 2 * 2 * N * N * B * F
-RG = {2: 4, 3: 4, 4: 3, 5: 4, 6: 3}
+RG = {2: 3, 3: 3, 4: 3, 5: 3, 6: 3}
 HALVED = (0, 1, 2, 3)
 
 

from contextlib import ExitStack

import concourse.mybir as mybir
from concourse.masks import make_identity

F32 = mybir.dt.float32
BF16 = mybir.dt.bfloat16
U32 = mybir.dt.uint32
U8 = mybir.dt.uint8
FP8X4 = mybir.dt.float8_e4m3fn_x4
MULT = mybir.AluOpType.mult
SUB = mybir.AluOpType.subtract

P = 128
B, N, F = 4, 2048, 128
NI = N // 256
NG = N // 512
FLOPS = 2 * 2 * N * N * B * F
RG = {2: 3, 3: 3, 4: 3, 5: 3, 6: 3}
HALVED = (0, 1, 2, 3)


def tile_gcncheb_pa_kernel(tc, x, L, out_0, out_1, out_2):
    nc = tc.nc
    with ExitStack() as ctx:
        ctx.enter_context(tc.manual_schedule())
        keep = ctx.enter_context(tc.tile_pool(name="keep", bufs=1))
        lgp = ctx.enter_context(tc.tile_pool(name="lgp", bufs=4))
        ldp = ctx.enter_context(tc.tile_pool(name="ldp", bufs=4))
        xgp = ctx.enter_context(tc.tile_pool(name="xgp", bufs=1))
        x1gp = ctx.enter_context(tc.tile_pool(name="x1gp", bufs=2))
        st1p = ctx.enter_context(tc.tile_pool(name="st1p", bufs=4))
        st2p = ctx.enter_context(tc.tile_pool(name="st2p", bufs=4))
        st3p = ctx.enter_context(tc.tile_pool(name="st3p", bufs=4))
        psum = ctx.enter_context(tc.psum_pool(name="psum", bufs=1))

        def bank(k, shape):
            return psum.tile(shape, F32, name="bank%d" % k, tag="bank%d" % k)

        ident = keep.tile([P, P], F32, name="ident", align_bytes=256)
        make_identity(nc, ident[:])

        lraw = [keep.tile([P, 2, N], BF16, name="lraw%d" % i, align_bytes=256) for i in range(NI)]
        xraw = keep.tile([P, B, N], BF16, name="xraw", align_bytes=256)
        ltc = keep.tile([P, NI, 2, 512], U32, name="ltc", align_bytes=256)
        lts = keep.tile([P, NI, 2, 512], U8, name="lts", align_bytes=256)
        xqc = keep.tile([P, 2, NG, 256], U32, name="xqc", align_bytes=256)
        xqs = keep.tile([P, 2, NG, 256], U8, name="xqs", align_bytes=256)
        yqc = keep.tile([P, 2, NG, 256], U32, name="yqc", align_bytes=256)
        yqs = keep.tile([P, 2, NG, 256], U8, name="yqs", align_bytes=256)

        def load_l(i):
            g0 = 512 * (i // 2)
            rows = L[g0 : g0 + 512, :].rearrange("(p w e) b -> p w e b", w=2, e=2)[:, i % 2]
            if i in HALVED:
                for e in range(2):
                    nc.sync.dma_start(out=lraw[i][:, e], in_=rows[:, e])
            else:
                nc.sync.dma_start(out=lraw[i][:], in_=rows)

        def load_x(c):
            nc.sync.dma_start(
                out=xraw[:, c, :].rearrange("p (g t f) -> p g t f", t=4, f=F),
                in_=x[c].rearrange("(g p t) f -> p g t f", p=P, t=4),
            )

        load_l(0)
        load_x(0)
        load_x(1)
        for i in range(1, NI):
            load_l(i)
        load_x(2)
        load_x(3)

        xg_tiles = {}

        def x_regroup(c):
            h, c2 = divmod(c, 2)
            if c2 == 0:
                xg = xgp.tile([P, NG, 2, F, 4], BF16, name="xg", align_bytes=256)
                xg_tiles[h] = xg
            src = xraw[:, c, :].rearrange("p (g t f i) -> p g f t i", t=4, f=F // 4, i=4)
            dst = xg_tiles[h][:, :, c2, :, :].rearrange("p g (f i) t -> p g f t i", i=4)
            if c % 2 == 1:
                nc.scalar.copy(out=dst[:, 2:4], in_=src[:, 2:4])
                nc.vector.tensor_copy(out=dst[:, 0:2], in_=src[:, 0:2])
            else:
                nc.vector.tensor_copy(out=dst, in_=src)

        def x_quant(h):
            nc.vector.quantize_mx(
                out=xqc[:, h].rearrange("p g w -> p (g w)").bitcast(FP8X4),
                scales=xqs[:, h].rearrange("p g w -> p (g w)"),
                in_=xg_tiles[h][:].rearrange("p g c f t -> p (g c f t)"),
            )

        ld_tiles = {}

        def reorder(i):
            for e in range(2):
                ld = ldp.tile([P, 2, P * RG[i]], F32, name="ld", align_bytes=256)
                ld_tiles[(i, e)] = ld
                nc.vector.tensor_copy(
                    out=ld[:],
                    in_=lraw[i][:, e, 0 : 512 * RG[i]].bitcast(F32).rearrange("p (w u) -> p u w", u=2),
                )

        lg_tiles = {}

        def transposes(i):
            for e in range(2):
                lw = lraw[i][:, e, :].bitcast(F32)
                lg = lgp.tile([P, N], BF16, name="lg", align_bytes=256)
                lg_tiles[(i, e)] = lg
                lgw = lg[:].bitcast(F32).rearrange("p (g c u) -> p g c u", c=P, u=2)
                for gg in range(2):
                    tp = bank(2 * e + gg, [P, 4, P])
                    for s in range(4):
                        g, u = 2 * gg + s // 2, s % 2
                        if g < RG.get(i, 0):
                            words = ld_tiles[(i, e)][:, u, P * g : P * g + P]
                        else:
                            words = lw[:, 256 * g + u : 256 * g + 256 : 2]
                        nc.tensor.transpose(tp[:, s, :], words, ident[:])
                    src = tp[:].rearrange("p (g u) c -> p g c u", u=2)
                    dst = lgw[:, 2 * gg : 2 * gg + 2, :, :]
                    if i == NI - 1 and e == 0 and gg == 1:
                        nc.vector.tensor_copy(out=dst, in_=src)
                    else:
                        nc.scalar.copy(out=dst, in_=src)

        def l_quant(i):
            for e in range(2):
                nc.vector.quantize_mx(
                    out=ltc[:, i, e, :].bitcast(FP8X4),
                    scales=lts[:, i, e, :],
                    in_=lg_tiles[(i, e)][:],
                )

        def one_pass(out, i, e, g, h, rc, rs):
            nc.tensor.matmul_mx(
                out=out,
                lhsT=ltc[:, i, e, P * g : P * g + P].bitcast(FP8X4),
                lhsT_scale=lts[:, i, e, P * g : P * g + P],
                rhs=rc[:, h, g, :].bitcast(FP8X4),
                rhs_scale=rs[:, h, g, :],
                start=(g == 0),
                stop=(g == NG - 1),
            )

        def passes(k, i, h, rc, rs):
            acc = bank(k, [P, 2, 256])
            for e in range(2):
                for g in range(NG):
                    one_pass(acc[:, e, :], i, e, g, h, rc, rs)
            return acc

        def dram_rows(o, g, h):
            return o[2 * h : 2 * h + 2, 512 * g : 512 * g + 512, :].rearrange(
                "c (p t) f -> p c (t f)", t=4
            )

        def tile_part(s, i):
            return s[:, :, 256 * (i % 2) : 256 * (i % 2) + 256]

        def empty(s, i, acc):
            nc.scalar.copy(
                out=tile_part(s, i).rearrange("p c (e f) -> p c e f", f=F),
                in_=acc[:].rearrange("p e (c f) -> p c e f", f=F),
            )

        st1_tiles = {}

        def hop1(k, i, h):
            acc = passes(k, i, h, xqc, xqs)
            g, w = divmod(i, 2)
            if w == 0:
                st1 = st1p.tile([P, 2, 512], F32, name="st1", align_bytes=256)
                st1_tiles[(g, h)] = st1
            empty(st1_tiles[(g, h)], i, acc)
            if w == 1:
                nc.sync.dma_start(out=dram_rows(out_0, g, h), in_=st1_tiles[(g, h)][:])

        x1g_tiles = {}

        def x1_regroup(g, h):
            x1g = x1gp.tile([P, 2, F, 4], BF16, name="x1g", align_bytes=256)
            x1g_tiles[(g, h)] = x1g
            nc.vector.tensor_copy(
                out=x1g[:].rearrange("p c (f i) t -> p c f t i", i=4),
                in_=st1_tiles[(g, h)][:].rearrange("p c (t f i) -> p c f t i", t=4, i=4),
            )

        def x1_quant(g, h):
            nc.vector.quantize_mx(
                out=yqc[:, h, g, :].bitcast(FP8X4),
                scales=yqs[:, h, g, :],
                in_=x1g_tiles[(g, h)][:].rearrange("p c f t -> p (c f t)"),
            )

        st2_tiles = {}
        st3_tiles = {}

        def stage2(g, h):
            st2 = st2p.tile([P, 2, 512], F32, name="st2", align_bytes=256)
            st3 = st3p.tile([P, 2, 512], F32, name="st3", align_bytes=256)
            st2_tiles[(g, h)] = st2
            st3_tiles[(g, h)] = st3

        def xt2(i, h):
            g, w = divmod(i, 2)
            nc.vector.scalar_tensor_tensor(
                out=tile_part(st3_tiles[(g, h)], i),
                in0=tile_part(st2_tiles[(g, h)], i),
                scalar=2.0,
                in1=xraw[:, 2 * h : 2 * h + 2, 256 * i : 256 * i + 256],
                op0=MULT,
                op1=SUB,
            )

        def store2(g, h, o, tiles):
            queue = nc.scalar if tiles is st2_tiles else nc.sync
            queue.dma_start(out=dram_rows(o, g, h), in_=tiles[(g, h)][:])

        def hop2(k, i, h):
            acc = passes(k, i, h, yqc, yqs)
            g, w = divmod(i, 2)
            if w == 0:
                stage2(g, h)
            empty(st2_tiles[(g, h)], i, acc)
            if w == 1:
                store2(g, h, out_1, st2_tiles)
            xt2(i, h)
            if w == 1:
                store2(g, h, out_2, st3_tiles)

        def warm(n):
            for r in range(n):
                w = bank(4 + r % 4, [P, 512])
                nc.tensor.matmul(
                    out=w[:], lhsT=xraw[:, 0, 0:P], rhs=xraw[:, 0, 0:512], start=True, stop=True
                )

        transposes(0)
        warm(6)
        x_regroup(0)
        l_quant(0)
        x_regroup(1)
        x_quant(0)
        for i in range(NI):
            if i + 1 < NI:
                transposes(i + 1)
            hop1(4 + i % 4, i, 0)
            if i + 2 in RG:
                reorder(i + 2)
            x1_ready = i // 2 - 1 if i % 2 == 0 and 0 < i else -1
            if x1_ready >= 0:
                x1_regroup(x1_ready, 0)
            if i + 1 < NI:
                l_quant(i + 1)
            if x1_ready >= 0:
                x1_quant(x1_ready, 0)
            if i == NI - 2:
                x_regroup(2)

        n_open = 3
        opened = {}
        for j in range(n_open):
            for e in range(2):
                acc = bank(2 * j + e, [P, 256])
                opened[(j, e)] = acc
                for g in range(NG - 1):
                    one_pass(acc[:], j, e, g, 0, yqc, yqs)
        x1_regroup(3, 0)
        x1_quant(3, 0)
        x_regroup(3)
        for j in range(n_open):
            g, w = divmod(j, 2)
            if w == 0:
                stage2(g, 0)
            for e in range(2):
                one_pass(opened[(j, e)][:], j, e, NG - 1, 0, yqc, yqs)
                nc.scalar.copy(
                    out=tile_part(st2_tiles[(g, 0)], j)[:, :, F * e : F * e + F],
                    in_=opened[(j, e)][:].rearrange("p (c f) -> p c f", f=F),
                )
            if w == 1:
                store2(g, 0, out_1, st2_tiles)
        xt2(0, 0)
        xt2(1, 0)
        store2(0, 0, out_2, st3_tiles)
        x_quant(1)
        xt2(2, 0)

        used = [2 * n_open]

        def next_bank():
            k = used[0] % 8
            used[0] += 1
            return k

        for j in range(n_open, 6):
            hop2(next_bank(), j, 0)
        for i in range(NI):
            hop1(next_bank(), i, 1)
            if i % 2 == 1:
                x1_regroup(i // 2, 1)
                x1_quant(i // 2, 1)
        for j in range(6, NI):
            hop2(next_bank(), j, 0)

        for j in range(NI):
            hop2(next_bank(), j, 1)
